import numpy as np
import ml_dtypes


def mxq(x, axis, fmt="e4m3"):
    dtype, down = {"e4m3": (ml_dtypes.float8_e4m3fn, 7), "e5m2": (ml_dtypes.float8_e5m2, 14)}[fmt]
    v = np.moveaxis(np.asarray(x, np.float32).astype(ml_dtypes.bfloat16).astype(np.float64), axis, -1)
    blocks = v.reshape(v.shape[:-1] + (-1, 32))
    amax = np.abs(blocks).max(-1, keepdims=True)
    byte = np.maximum(np.where(amax > 0, np.frexp(amax)[1] - 1 + 127, 0) - down, 1)
    scale = np.exp2(byte - 127.0)
    codes = (blocks / scale).astype(np.float32).astype(dtype).astype(np.float64)
    return np.moveaxis((codes * scale).reshape(v.shape), -1, axis)


WIDE = False


def mx_kscale(k):
    if not WIDE:
        return np.ones(k)
    levels = np.array([10, -10, 5, -5, 0])
    a = np.random.permutation(np.resize(levels, k // 512 * 4)).reshape(k // 512, 4)
    idx = np.arange(k)
    return np.exp2(a[idx // 512, idx % 128 // 32])


BF16 = ml_dtypes.bfloat16


def bf(x):
    return np.asarray(x, np.float32).astype(BF16)


def f64(x):
    return np.asarray(x).astype(np.float64)


B, T, C, NH, NC = 2, 2048, 512, 4, 2
HS = C // NH
N = T // NC


def setup_inputs():
    s = mx_kscale(C)
    t = mx_kscale(T)
    return {"x": bf(np.random.standard_normal((B, T, C)) * s * t[:, None]),
            "Wk": bf(np.random.standard_normal((C, C)) / np.sqrt(C) / s),
            "pk_W": bf(np.random.standard_normal((NC, N, N)) / np.sqrt(N) / t.reshape(NC, 1, N)),
            "pk_b": bf(np.random.standard_normal((NC, N)) * 0.3)}


def reference(x, Wk, pk_W, pk_b):
    kh = mxq(f64(x), 2, "e4m3") @ mxq(f64(Wk), 1, "e4m3").T
    kh = kh.reshape(B, T, NH, HS).transpose(0, 2, 1, 3).reshape(B, NH, NC, N, HS)
    out = (mxq(f64(pk_W), 2, "e4m3") @ mxq(kh, 3, "e4m3")) + f64(pk_b)[:, :, None]
    return out.reshape(B, NH, T, HS)

@@ -1,0 +1,177 @@
+from contextlib import ExitStack
+
+import concourse.mybir as mybir
+from concourse.masks import make_identity
+
+F32 = mybir.dt.float32
+BF16 = mybir.dt.bfloat16
+U32 = mybir.dt.uint32
+U8 = mybir.dt.uint8
+FP8X4 = mybir.dt.float8_e4m3fn_x4
+IDENTITY = mybir.ActivationFunctionType.Identity
+
+P = 128
+B, T, C, NH, NC = 2, 2048, 512, 4, 2
+HS = C // NH
+N = T // NC
+FLOPS = 2 * B * T * C * C + 2 * B * NH * NC * N * N * HS
+
+MANUAL = True
+
+LOADS = ["W", "X0", "X1", "P0", "P1", "P2", "P3", "X2", "X3", "X4", "P4", "X5", "P5", "X6", "P6", "X7", "P7"]
+ORDER = ["W", "X0", "X1", "K0", "P0", "K1", "P1", "P2", "P3", "X2", "U0", "X3", "K2", "U1", "X4", "P4", "K3",
+         "X5", "P5", "K4", "U2", "X6", "P6", "K5", "U3", "X7", "P7", "K6", "U4", "K7", "U5", "U6", "U7"]
+
+
+def tile_causalselfattention_pa_t_kernel(tc, x, Wk, pk_W, pk_b, out):
+    nc = tc.nc
+    with ExitStack() as ctx:
+        if MANUAL:
+            ctx.enter_context(tc.manual_schedule())
+        consts = ctx.enter_context(tc.tile_pool(name="consts", bufs=1))
+        inputs = ctx.enter_context(tc.tile_pool(name="inputs", bufs=1))
+        keep = ctx.enter_context(tc.tile_pool(name="keep", bufs=1))
+        grouped = ctx.enter_context(tc.tile_pool(name="grouped", bufs=6))
+        staging = ctx.enter_context(tc.tile_pool(name="staging", bufs=4))
+        psum = ctx.enter_context(tc.psum_pool(name="psum", bufs=8))
+
+        warm_in = consts.tile([P, 1], F32)
+        warm_out = consts.tile([P, 1], F32)
+        nc.vector.memset(warm_in[:], 0.0)
+        nc.scalar.activation(out=warm_out[:], in_=warm_in[:], func=IDENTITY)
+        ident = consts.tile([P, P], F32)
+        make_identity(nc, ident[:])
+        bias_bf = consts.tile([P, NC * 8], BF16)
+        bias = consts.tile([P, NC * 8], F32)
+        nc.scalar.dma_start(out=bias_bf[:].rearrange("p (c j) -> p c j", c=NC),
+                            in_=pk_b.rearrange("c (p j) -> p c j", j=8))
+
+        src = {}
+        for unit in LOADS:
+            kind, n = unit[0], int(unit[1:] or 0)
+            raw = inputs.tile([P, 2048], BF16, name="raw_" + unit)
+            src[unit] = raw
+            if kind == "W":
+                nc.sync.dma_start(out=raw[:].rearrange("p (i c) -> p i c", i=4),
+                                  in_=Wk.rearrange("(i p) c -> p i c", p=P))
+            elif kind == "X":
+                b, c, g2 = (n // 2) % 2, n // 4, n % 2
+                t0 = N * c + 512 * g2
+                nc.sync.dma_start(out=raw[:].rearrange("p (a w) -> p a w", a=2),
+                                  in_=x[b, t0:t0 + 512, :].rearrange("(a p e) c -> p a (e c)", a=2, p=P, e=2))
+            else:
+                c, jj = n // 4, n % 4
+                nc.sync.dma_start(out=raw[:],
+                                  in_=pk_W[c].rearrange("(p j) n -> p (j n)", j=8)[:, 2048 * jj:2048 * jj + 2048])
+
+        codes = {}
+        scales = {}
+        count = {"V": 0, "S": 0}
+        waiting = []
+
+        def quantise(entry):
+            unit, grp = entry[0], entry[1]
+            cw = keep.tile([P, 512], U32, name="codes_" + unit, align_bytes=64)
+            sc = keep.tile([P, 512], U8, name="scales_" + unit, align_bytes=64)
+            nc.vector.quantize_mx(out=cw[:].bitcast(FP8X4), scales=sc[:], in_=grp[:])
+            codes[unit] = cw
+            scales[unit] = sc
+            count["V"] += 1
+
+        def flush(needed):
+            due = [entry for entry in waiting if entry[2] <= 0 or entry[0] in needed]
+            waiting[:] = [entry for entry in waiting if not (entry[2] <= 0 or entry[0] in needed)]
+            for entry in due:
+                quantise(entry)
+
+        def pick():
+            eng = "S" if count["S"] <= count["V"] + len(waiting) else "V"
+            count[eng] += 1
+            return eng
+
+        def passed():
+            for entry in waiting:
+                entry[2] -= 1
+            flush([])
+
+        def copy(eng, dst, srcap):
+            if eng == "V":
+                nc.vector.tensor_copy(out=dst, in_=srcap)
+            else:
+                nc.scalar.copy(out=dst, in_=srcap)
+
+        bias_done = [False]
+
+        for unit in ORDER:
+            kind, n = unit[0], int(unit[1:] or 0)
+            if kind in "WXP":
+                words = src[unit][:].bitcast(F32)
+                banks = []
+                for k in range(2):
+                    bank = psum.tile([P, 4, P], F32, name="bank", tag="bank")
+                    for s in range(4):
+                        col = 512 * k + 128 * s
+                        nc.tensor.transpose(bank[:, s, :], words[:, col:col + 128], ident[:])
+                    banks.append(bank)
+                grp = grouped.tile([P, 2048], BF16, name="grp", tag="grp", align_bytes=64)
+                gw = grp[:].bitcast(F32)
+                for k in range(2):
+                    copy(pick(), gw[:, 512 * k:512 * k + 512].rearrange("q (i o u) -> q i o u", i=2, u=2),
+                         banks[k][:].rearrange("q (i u) o -> q i o u", i=2))
+                    passed()
+                waiting.append([unit, grp, 1])
+            elif kind == "K":
+                flush(["W", "X%d" % n])
+                xq, xs, wq, ws = codes["X%d" % n], scales["X%d" % n], codes["W"], scales["W"]
+                banks = []
+                for h in range(NH):
+                    bank = psum.tile([P, 4, P], F32, name="bank", tag="bank")
+                    for t in range(4):
+                        nc.tensor.matmul_mx(out=bank[:, t, :],
+                                            lhsT=xq[:, 128 * t:128 * t + 128].bitcast(FP8X4),
+                                            lhsT_scale=xs[:, 128 * t:128 * t + 128],
+                                            rhs=wq[:, 128 * h:128 * h + 128].bitcast(FP8X4),
+                                            rhs_scale=ws[:, 128 * h:128 * h + 128],
+                                            start=True, stop=True)
+                    banks.append(bank)
+                grp = grouped.tile([P, 2048], BF16, name="grp", tag="grp", align_bytes=64)
+                for h in range(NH):
+                    copy(pick(), grp[:, 512 * h:512 * h + 512].rearrange("p (d t) -> p d t", t=4),
+                         banks[h][:].rearrange("p t d -> p d t"))
+                    passed()
+                waiting.append([unit, grp, 1])
+            else:
+                bc, c, half = n // 2, n // 4, n % 2
+                b = bc % 2
+                pk_units = ["P%d" % (4 * c + 2 * half), "P%d" % (4 * c + 2 * half + 1)]
+                kh_units = ["K%d" % (2 * bc), "K%d" % (2 * bc + 1)]
+                flush(pk_units + kh_units)
+                if not bias_done[0]:
+                    nc.vector.tensor_copy(out=bias[:], in_=bias_bf[:])
+                    bias_done[0] = True
+                banks = []
+                for i in range(4):
+                    pq, ps = codes[pk_units[i // 2]], scales[pk_units[i // 2]]
+                    bank = psum.tile([P, 512], F32, name="bank", tag="bank")
+                    for g2 in range(2):
+                        col = 256 * (i % 2) + 128 * g2
+                        nc.tensor.matmul_mx(out=bank[:],
+                                            lhsT=pq[:, col:col + 128].bitcast(FP8X4),
+                                            lhsT_scale=ps[:, col:col + 128],
+                                            rhs=codes[kh_units[g2]][:].bitcast(FP8X4),
+                                            rhs_scale=scales[kh_units[g2]][:],
+                                            start=(g2 == 0), stop=(g2 == 1))
+                    banks.append(bank)
+                res = staging.tile([P, NH, 4, HS], F32, name="res", tag="res")
+                for i in range(4):
+                    j = 4 * half + i
+                    acc = banks[i][:].rearrange("p (h d) -> p h d", h=NH)
+                    col = 8 * c + j
+                    if pick() == "V":
+                        nc.vector.tensor_scalar_add(out=res[:, :, i, :], in0=acc, scalar1=bias[:, col:col + 1])
+                    else:
+                        nc.scalar.activation(out=res[:, :, i, :], in_=acc, func=IDENTITY,
+                                             bias=bias[:, col:col + 1], scale=1.0)
+                    passed()
+                dst = out[b, :, N * c:N * c + N, :].rearrange("h (p j) d -> p h j d", j=8)
+                nc.sync.dma_start(out=dst[:, :, 4 * half:4 * half + 4, :], in_=res[:])

@@ -18,9 +18,10 @@ FLOPS = 2 * B * T * C * C + 2 * B * NH * NC * N * N * HS
 
 MANUAL = True
 
-LOADS = ["W", "X0", "X1", "P0", "P1", "P2", "P3", "X2", "X3", "X4", "P4", "X5", "P5", "X6", "P6", "X7", "P7"]
-ORDER = ["W", "X0", "X1", "K0", "P0", "K1", "P1", "P2", "P3", "X2", "U0", "X3", "K2", "U1", "X4", "P4", "K3",
-         "X5", "P5", "K4", "U2", "X6", "P6", "K5", "U3", "X7", "P7", "K6", "U4", "K7", "U5", "U6", "U7"]
+ORDER = ["X0", "W", "X1", "P0", "K0", "K1", "P1", "P2", "P3", "X2", "S000", "S010", "X3", "X4", "X5",
+         "S020", "S030", "K2", "K3", "K4", "X6", "X7", "P4", "S001", "S011", "K5", "S021", "S031", "K6",
+         "P5", "P6", "P7", "S100", "S110", "K7", "S120", "S130", "S101", "S111", "S121", "S131"]
+PAIR_STORES = ["S121", "S131"]
 
 
 def tile_causalselfattention_pa_t_kernel(tc, x, Wk, pk_W, pk_b, out):
@@ -47,7 +48,7 @@ def tile_causalselfattention_pa_t_kernel(tc, x, Wk, pk_W, pk_b, out):
                             in_=pk_b.rearrange("c (p j) -> p c j", j=8))
 
         src = {}
-        for unit in LOADS:
+        for unit in [u for u in ORDER if u[0] in "WXP"]:
             kind, n = unit[0], int(unit[1:] or 0)
             raw = inputs.tile([P, 2048], BF16, name="raw_" + unit)
             src[unit] = raw
@@ -101,6 +102,7 @@ def tile_causalselfattention_pa_t_kernel(tc, x, Wk, pk_W, pk_b, out):
                 nc.scalar.copy(out=dst, in_=srcap)
 
         bias_done = [False]
+        results = {}
 
         for unit in ORDER:
             kind, n = unit[0], int(unit[1:] or 0)
@@ -141,20 +143,20 @@ def tile_causalselfattention_pa_t_kernel(tc, x, Wk, pk_W, pk_b, out):
                     passed()
                 waiting.append([unit, grp, 1])
             else:
-                bc, c, half = n // 2, n // 4, n % 2
-                b = bc % 2
-                pk_units = ["P%d" % (4 * c + 2 * half), "P%d" % (4 * c + 2 * half + 1)]
+                c, jj, b = int(unit[1]), int(unit[2]), int(unit[3])
+                bc = 2 * c + b
+                pk_unit = "P%d" % (4 * c + jj)
                 kh_units = ["K%d" % (2 * bc), "K%d" % (2 * bc + 1)]
-                flush(pk_units + kh_units)
+                flush([pk_unit] + kh_units)
                 if not bias_done[0]:
                     nc.vector.tensor_copy(out=bias[:], in_=bias_bf[:])
                     bias_done[0] = True
+                pq, ps = codes[pk_unit], scales[pk_unit]
                 banks = []
-                for i in range(4):
-                    pq, ps = codes[pk_units[i // 2]], scales[pk_units[i // 2]]
+                for i in range(2):
                     bank = psum.tile([P, 512], F32, name="bank", tag="bank")
                     for g2 in range(2):
-                        col = 256 * (i % 2) + 128 * g2
+                        col = 256 * i + 128 * g2
                         nc.tensor.matmul_mx(out=bank[:],
                                             lhsT=pq[:, col:col + 128].bitcast(FP8X4),
                                             lhsT_scale=ps[:, col:col + 128],
@@ -162,16 +164,26 @@ def tile_causalselfattention_pa_t_kernel(tc, x, Wk, pk_W, pk_b, out):
                                             rhs_scale=scales[kh_units[g2]][:],
                                             start=(g2 == 0), stop=(g2 == 1))
                     banks.append(bank)
-                res = staging.tile([P, NH, 4, HS], F32, name="res", tag="res")
-                for i in range(4):
-                    j = 4 * half + i
+                half = jj // 2
+                key = (c, b, half)
+                if key not in results:
+                    res = staging.tile([P, NH, 4, HS], F32, name="res", tag="res")
+                    results[key] = [res, 0]
+                res = results[key][0]
+                results[key][1] += 1
+                for i in range(2):
+                    j = 2 * jj + i
                     acc = banks[i][:].rearrange("p (h d) -> p h d", h=NH)
                     col = 8 * c + j
                     if pick() == "V":
-                        nc.vector.tensor_scalar_add(out=res[:, :, i, :], in0=acc, scalar1=bias[:, col:col + 1])
+                        nc.vector.tensor_scalar_add(out=res[:, :, j % 4, :], in0=acc, scalar1=bias[:, col:col + 1])
                     else:
-                        nc.scalar.activation(out=res[:, :, i, :], in_=acc, func=IDENTITY,
+                        nc.scalar.activation(out=res[:, :, j % 4, :], in_=acc, func=IDENTITY,
                                              bias=bias[:, col:col + 1], scale=1.0)
                     passed()
                 dst = out[b, :, N * c:N * c + N, :].rearrange("h (p j) d -> p h j d", j=8)
-                nc.sync.dma_start(out=dst[:, :, 4 * half:4 * half + 4, :], in_=res[:])
+                if unit in PAIR_STORES:
+                    lo = 2 * (jj % 2)
+                    nc.sync.dma_start(out=dst[:, :, 2 * jj:2 * jj + 2, :], in_=res[:, :, lo:lo + 2, :])
+                elif results[key][1] == 2:
+                    nc.sync.dma_start(out=dst[:, :, 4 * half:4 * half + 4, :], in_=res[:])

@@ -16,23 +16,23 @@ HS = C // NH
 N = T // NC
 FLOPS = 2 * B * T * C * C + 2 * B * NH * NC * N * N * HS
 
-MANUAL = True
-
-ORDER = ["X0", "W", "X1", "P0", "K0", "K1", "P1", "P2", "P3", "X2", "S000", "S010", "X3", "X4", "X5",
-         "S020", "S030", "K2", "K3", "K4", "X6", "X7", "P4", "S001", "S011", "K5", "S021", "S031", "K6",
-         "P5", "P6", "P7", "S100", "S110", "K7", "S120", "S130", "S101", "S111", "S121", "S131"]
+UNITS = ["X0", "W", "X1", "P0", "P1", "K0", "K1", "P2", "P3", "X2", "X3", "X4", "S000", "S010", "S020",
+          "S030", "K2", "K3", "K4", "X5", "X6", "X7", "P4", "P5", "P6", "P7", "S001", "S011", "K5", "S021",
+          "S031", "K6", "K7", "S100", "S110", "S120", "S130", "S101", "S111", "S121", "S131"]
+STEPS = ("ppvsppvsqppvsqppvsqppvpspqpspvpspqpspvpsvpspqpspqpspvsppqspqpsvpsqpsqpspvspqspvspvspvpspvp"
+         "spvpspvpspqpspvpspvpsqpsppqspvpspqpspqpspvspqpspqspvspqspqspvsppqsppvspvspvspvspqsppvsppvs"
+         "ppvsppqspvspvpsqpspvpspvpspvpspvpspvpspvs")
 PAIR_STORES = ["S121", "S131"]
 
 
 def tile_causalselfattention_pa_t_kernel(tc, x, Wk, pk_W, pk_b, out):
     nc = tc.nc
     with ExitStack() as ctx:
-        if MANUAL:
-            ctx.enter_context(tc.manual_schedule())
+        ctx.enter_context(tc.manual_schedule())
         consts = ctx.enter_context(tc.tile_pool(name="consts", bufs=1))
         inputs = ctx.enter_context(tc.tile_pool(name="inputs", bufs=1))
         keep = ctx.enter_context(tc.tile_pool(name="keep", bufs=1))
-        grouped = ctx.enter_context(tc.tile_pool(name="grouped", bufs=6))
+        grouped = ctx.enter_context(tc.tile_pool(name="grouped", bufs=8))
         staging = ctx.enter_context(tc.tile_pool(name="staging", bufs=4))
         psum = ctx.enter_context(tc.psum_pool(name="psum", bufs=8))
 
@@ -48,7 +48,7 @@ def tile_causalselfattention_pa_t_kernel(tc, x, Wk, pk_W, pk_b, out):
                             in_=pk_b.rearrange("c (p j) -> p c j", j=8))
 
         src = {}
-        for unit in [u for u in ORDER if u[0] in "WXP"]:
+        for unit in [u for u in UNITS if u[0] in "WXP"]:
             kind, n = unit[0], int(unit[1:] or 0)
             raw = inputs.tile([P, 2048], BF16, name="raw_" + unit)
             src[unit] = raw
@@ -64,126 +64,114 @@ def tile_causalselfattention_pa_t_kernel(tc, x, Wk, pk_W, pk_b, out):
                 c, jj = n // 4, n % 4
                 nc.sync.dma_start(out=raw[:],
                                   in_=pk_W[c].rearrange("(p j) n -> p (j n)", j=8)[:, 2048 * jj:2048 * jj + 2048])
-
         codes = {}
         scales = {}
-        count = {"V": 0, "S": 0}
-        waiting = []
+        groups = {}
+        results = {}
+        todo = [(unit, k) for unit in UNITS for k in range(4 if unit[0] == "K" else 2)]
+        filled = []
+        to_quantise = []
+        done = {"p": 0, "e": 0, "q": 0}
 
-        def quantise(entry):
-            unit, grp = entry[0], entry[1]
-            cw = keep.tile([P, 512], U32, name="codes_" + unit, align_bytes=64)
-            sc = keep.tile([P, 512], U8, name="scales_" + unit, align_bytes=64)
-            nc.vector.quantize_mx(out=cw[:].bitcast(FP8X4), scales=sc[:], in_=grp[:])
-            codes[unit] = cw
-            scales[unit] = sc
-            count["V"] += 1
-
-        def flush(needed):
-            due = [entry for entry in waiting if entry[2] <= 0 or entry[0] in needed]
-            waiting[:] = [entry for entry in waiting if not (entry[2] <= 0 or entry[0] in needed)]
-            for entry in due:
-                quantise(entry)
-
-        def pick():
-            eng = "S" if count["S"] <= count["V"] + len(waiting) else "V"
-            count[eng] += 1
-            return eng
-
-        def passed():
-            for entry in waiting:
-                entry[2] -= 1
-            flush([])
+        def fill(unit, k):
+            kind, n = unit[0], int(unit[1:] or 0)
+            if kind in "WXP":
+                bank = psum.tile([P, 4, P], F32, name="bank", tag="bank")
+                for s in range(4):
+                    col = 512 * k + 128 * s
+                    nc.tensor.transpose(bank[:, s, :], src[unit][:].bitcast(F32)[:, col:col + 128], ident[:])
+            elif kind == "K":
+                xq, xs, wq, ws = codes["X%d" % n], scales["X%d" % n], codes["W"], scales["W"]
+                bank = psum.tile([P, 4, P], F32, name="bank", tag="bank")
+                for t in range(4):
+                    nc.tensor.matmul_mx(out=bank[:, t, :],
+                                        lhsT=xq[:, 128 * t:128 * t + 128].bitcast(FP8X4),
+                                        lhsT_scale=xs[:, 128 * t:128 * t + 128],
+                                        rhs=wq[:, 128 * k:128 * k + 128].bitcast(FP8X4),
+                                        rhs_scale=ws[:, 128 * k:128 * k + 128],
+                                        start=True, stop=True)
+            else:
+                c, jj, b = int(unit[1]), int(unit[2]), int(unit[3])
+                if not results:
+                    nc.vector.tensor_copy(out=bias[:], in_=bias_bf[:])
+                    results["bias"] = True
+                pq, ps = codes["P%d" % (4 * c + jj)], scales["P%d" % (4 * c + jj)]
+                bank = psum.tile([P, 512], F32, name="bank", tag="bank")
+                for g2 in range(2):
+                    kh = "K%d" % (2 * (2 * c + b) + g2)
+                    col = 256 * k + 128 * g2
+                    nc.tensor.matmul_mx(out=bank[:],
+                                        lhsT=pq[:, col:col + 128].bitcast(FP8X4),
+                                        lhsT_scale=ps[:, col:col + 128],
+                                        rhs=codes[kh][:].bitcast(FP8X4),
+                                        rhs_scale=scales[kh][:],
+                                        start=(g2 == 0), stop=(g2 == 1))
+            filled.append((unit, k, bank))
 
         def copy(eng, dst, srcap):
-            if eng == "V":
+            if eng == "v":
                 nc.vector.tensor_copy(out=dst, in_=srcap)
             else:
                 nc.scalar.copy(out=dst, in_=srcap)
 
-        bias_done = [False]
-        results = {}
-
-        for unit in ORDER:
-            kind, n = unit[0], int(unit[1:] or 0)
-            if kind in "WXP":
-                words = src[unit][:].bitcast(F32)
-                banks = []
-                for k in range(2):
-                    bank = psum.tile([P, 4, P], F32, name="bank", tag="bank")
-                    for s in range(4):
-                        col = 512 * k + 128 * s
-                        nc.tensor.transpose(bank[:, s, :], words[:, col:col + 128], ident[:])
-                    banks.append(bank)
-                grp = grouped.tile([P, 2048], BF16, name="grp", tag="grp", align_bytes=64)
-                gw = grp[:].bitcast(F32)
-                for k in range(2):
-                    copy(pick(), gw[:, 512 * k:512 * k + 512].rearrange("q (i o u) -> q i o u", i=2, u=2),
-                         banks[k][:].rearrange("q (i u) o -> q i o u", i=2))
-                    passed()
-                waiting.append([unit, grp, 1])
-            elif kind == "K":
-                flush(["W", "X%d" % n])
-                xq, xs, wq, ws = codes["X%d" % n], scales["X%d" % n], codes["W"], scales["W"]
-                banks = []
-                for h in range(NH):
-                    bank = psum.tile([P, 4, P], F32, name="bank", tag="bank")
-                    for t in range(4):
-                        nc.tensor.matmul_mx(out=bank[:, t, :],
-                                            lhsT=xq[:, 128 * t:128 * t + 128].bitcast(FP8X4),
-                                            lhsT_scale=xs[:, 128 * t:128 * t + 128],
-                                            rhs=wq[:, 128 * h:128 * h + 128].bitcast(FP8X4),
-                                            rhs_scale=ws[:, 128 * h:128 * h + 128],
-                                            start=True, stop=True)
-                    banks.append(bank)
-                grp = grouped.tile([P, 2048], BF16, name="grp", tag="grp", align_bytes=64)
-                for h in range(NH):
-                    copy(pick(), grp[:, 512 * h:512 * h + 512].rearrange("p (d t) -> p d t", t=4),
-                         banks[h][:].rearrange("p t d -> p d t"))
-                    passed()
-                waiting.append([unit, grp, 1])
+        def empty(eng):
+            unit, k, bank = filled[done["e"]]
+            done["e"] += 1
+            kind = unit[0]
+            if kind in "WXPK":
+                if k == 0:
+                    grp = grouped.tile([P, 2048], BF16, name="grp", tag="grp", align_bytes=64)
+                    groups[unit] = grp
+                grp = groups[unit]
+                if kind == "K":
+                    copy(eng, grp[:, 512 * k:512 * k + 512].rearrange("p (d t) -> p d t", t=4),
+                         bank[:].rearrange("p t d -> p d t"))
+                    if k == 3:
+                        to_quantise.append(unit)
+                else:
+                    copy(eng, grp[:].bitcast(F32)[:, 512 * k:512 * k + 512].rearrange("q (i o u) -> q i o u", i=2, u=2),
+                         bank[:].rearrange("q (i u) o -> q i o u", i=2))
+                    if k == 1:
+                        to_quantise.append(unit)
+                return
+            c, jj, b = int(unit[1]), int(unit[2]), int(unit[3])
+            half = jj // 2
+            key = (c, b, half)
+            if key not in results:
+                res = staging.tile([P, NH, 4, HS], F32, name="res", tag="res")
+                results[key] = [res, 0]
+            res = results[key][0]
+            results[key][1] += 1
+            j = 2 * jj + k
+            acc = bank[:].rearrange("p (h d) -> p h d", h=NH)
+            col = 8 * c + j
+            if eng == "v":
+                nc.vector.tensor_scalar_add(out=res[:, :, j % 4, :], in0=acc, scalar1=bias[:, col:col + 1])
             else:
-                c, jj, b = int(unit[1]), int(unit[2]), int(unit[3])
-                bc = 2 * c + b
-                pk_unit = "P%d" % (4 * c + jj)
-                kh_units = ["K%d" % (2 * bc), "K%d" % (2 * bc + 1)]
-                flush([pk_unit] + kh_units)
-                if not bias_done[0]:
-                    nc.vector.tensor_copy(out=bias[:], in_=bias_bf[:])
-                    bias_done[0] = True
-                pq, ps = codes[pk_unit], scales[pk_unit]
-                banks = []
-                for i in range(2):
-                    bank = psum.tile([P, 512], F32, name="bank", tag="bank")
-                    for g2 in range(2):
-                        col = 256 * i + 128 * g2
-                        nc.tensor.matmul_mx(out=bank[:],
-                                            lhsT=pq[:, col:col + 128].bitcast(FP8X4),
-                                            lhsT_scale=ps[:, col:col + 128],
-                                            rhs=codes[kh_units[g2]][:].bitcast(FP8X4),
-                                            rhs_scale=scales[kh_units[g2]][:],
-                                            start=(g2 == 0), stop=(g2 == 1))
-                    banks.append(bank)
-                half = jj // 2
-                key = (c, b, half)
-                if key not in results:
-                    res = staging.tile([P, NH, 4, HS], F32, name="res", tag="res")
-                    results[key] = [res, 0]
-                res = results[key][0]
-                results[key][1] += 1
-                for i in range(2):
-                    j = 2 * jj + i
-                    acc = banks[i][:].rearrange("p (h d) -> p h d", h=NH)
-                    col = 8 * c + j
-                    if pick() == "V":
-                        nc.vector.tensor_scalar_add(out=res[:, :, j % 4, :], in0=acc, scalar1=bias[:, col:col + 1])
-                    else:
-                        nc.scalar.activation(out=res[:, :, j % 4, :], in_=acc, func=IDENTITY,
-                                             bias=bias[:, col:col + 1], scale=1.0)
-                    passed()
-                dst = out[b, :, N * c:N * c + N, :].rearrange("h (p j) d -> p h j d", j=8)
-                if unit in PAIR_STORES:
+                nc.scalar.activation(out=res[:, :, j % 4, :], in_=acc, func=IDENTITY,
+                                     bias=bias[:, col:col + 1], scale=1.0)
+            dst = out[b, :, N * c:N * c + N, :].rearrange("h (p j) d -> p h j d", j=8)
+            if unit in PAIR_STORES:
+                if k == 1:
                     lo = 2 * (jj % 2)
                     nc.sync.dma_start(out=dst[:, :, 2 * jj:2 * jj + 2, :], in_=res[:, :, lo:lo + 2, :])
-                elif results[key][1] == 2:
-                    nc.sync.dma_start(out=dst[:, :, 4 * half:4 * half + 4, :], in_=res[:])
+            elif results[key][1] == 4:
+                nc.sync.dma_start(out=dst[:, :, 4 * half:4 * half + 4, :], in_=res[:])
+
+        def quantise():
+            unit = to_quantise[done["q"]]
+            done["q"] += 1
+            cw = keep.tile([P, 512], U32, name="codes_" + unit, align_bytes=64)
+            sc = keep.tile([P, 512], U8, name="scales_" + unit, align_bytes=64)
+            nc.vector.quantize_mx(out=cw[:].bitcast(FP8X4), scales=sc[:], in_=groups[unit][:])
+            codes[unit] = cw
+            scales[unit] = sc
+
+        for step in STEPS:
+            if step == "p":
+                fill(todo[done["p"]][0], todo[done["p"]][1])
+                done["p"] += 1
+            elif step == "q":
+                quantise()
+            else:
+                empty(step)

@@ -16,13 +16,13 @@ HS = C // NH
 N = T // NC
 FLOPS = 2 * B * T * C * C + 2 * B * NH * NC * N * N * HS
 
-UNITS = ["X0", "W", "X1", "P0", "P1", "K0", "K1", "P2", "P3", "X2", "X3", "X4", "S000", "S010", "S020",
-          "S030", "K2", "K3", "K4", "X5", "X6", "X7", "P4", "P5", "P6", "P7", "S001", "S011", "K5", "S021",
-          "S031", "K6", "K7", "S100", "S110", "S120", "S130", "S101", "S111", "S121", "S131"]
-STEPS = ("ppvsppvsqppvsqppvsqppvpspqpspvpspqpspvpsvpspqpspqpspvsppqspqpsvpsqpsqpspvspqspvspvspvpspvp"
-         "spvpspvpspqpspvpspvpsqpsppqspvpspqpspqpspvspqpspqspvspqspqspvsppqsppvspvspvspvspqsppvsppvs"
-         "ppvsppqspvspvpsqpspvpspvpspvpspvpspvpspvs")
-PAIR_STORES = ["S121", "S131"]
+UNITS = ["W", "X1", "X0", "P0", "X3", "K1", "K0", "P3", "P1", "K3", "X2", "P2", "S030", "S010", "P4", "X4",
+          "K2", "P6", "X5", "S020", "X6", "P5", "S021", "K5", "S001", "K6", "K4", "P7", "X7", "S000", "S011",
+          "S100", "S110", "K7", "S031", "S120", "S130", "S101", "S111", "S121", "S131"]
+STEPS = ("ppvsppvsqppvsqppvsqppvpspqpspvpspqpspvpsvpspqpspqsppvspqpspqsppvspvspqspqspvspqpspvpspvspp"
+         "vsppqspqsppvspvspqspqsppsqppsvpsvpsqppsqppsvpsvpsvppsqppsvpspvpspvpsqppsvpsqpsqpsvpsqpspvp"
+         "spvpspvpspvpspvpsqpspvpspvpspvpspvpspvpsv")
+PAIR_STORES = ["S010", "S021", "S000", "S031", "S121", "S131"]
 
 
 def tile_causalselfattention_pa_t_kernel(tc, x, Wk, pk_W, pk_b, out):
@@ -33,7 +33,7 @@ def tile_causalselfattention_pa_t_kernel(tc, x, Wk, pk_W, pk_b, out):
         inputs = ctx.enter_context(tc.tile_pool(name="inputs", bufs=1))
         keep = ctx.enter_context(tc.tile_pool(name="keep", bufs=1))
         grouped = ctx.enter_context(tc.tile_pool(name="grouped", bufs=8))
-        staging = ctx.enter_context(tc.tile_pool(name="staging", bufs=4))
+        staging = ctx.enter_context(tc.tile_pool(name="staging", bufs=6))
         psum = ctx.enter_context(tc.psum_pool(name="psum", bufs=8))
 
         warm_in = consts.tile([P, 1], F32)

@@ -5,6 +5,7 @@ from concourse.masks import make_identity
 
 F32 = mybir.dt.float32
 BF16 = mybir.dt.bfloat16
+I32 = mybir.dt.int32
 U32 = mybir.dt.uint32
 U8 = mybir.dt.uint8
 FP8X4 = mybir.dt.float8_e4m3fn_x4
@@ -16,13 +17,11 @@ HS = C // NH
 N = T // NC
 FLOPS = 2 * B * T * C * C + 2 * B * NH * NC * N * N * HS
 
-UNITS = ["W", "X1", "X0", "P0", "X3", "K1", "K0", "P3", "P1", "K3", "X2", "P2", "S030", "S010", "P4", "X4",
-          "K2", "P6", "X5", "S020", "X6", "P5", "S021", "K5", "S001", "K6", "K4", "P7", "X7", "S000", "S011",
-          "S100", "S110", "K7", "S031", "S120", "S130", "S101", "S111", "S121", "S131"]
-STEPS = ("ppvsppvsqppvsqppvsqppvpspqpspvpspqpspvpsvpspqpspqsppvspqpspqsppvspvspqspqspvspqpspvpspvspp"
-         "vsppqspqsppvspvspqspqsppsqppsvpsvpsqppsqppsvpsvpsvppsqppsvpspvpspvpsqppsvpsqpsqpsvpsqpspvp"
-         "spvpspvpspvpspvpsqpspvpspvpspvpspvpspvpsv")
-PAIR_STORES = ["S010", "S021", "S000", "S031", "S121", "S131"]
+GROUPS = 8
+MIXES = 16
+FIRST_MIX = 4
+ROUNDS = FIRST_MIX + MIXES // 2
+LAG = 2
 
 
 def tile_causalselfattention_pa_t_kernel(tc, x, Wk, pk_W, pk_b, out):
@@ -32,14 +31,14 @@ def tile_causalselfattention_pa_t_kernel(tc, x, Wk, pk_W, pk_b, out):
         consts = ctx.enter_context(tc.tile_pool(name="consts", bufs=1))
         inputs = ctx.enter_context(tc.tile_pool(name="inputs", bufs=1))
         keep = ctx.enter_context(tc.tile_pool(name="keep", bufs=1))
-        grouped = ctx.enter_context(tc.tile_pool(name="grouped", bufs=8))
-        staging = ctx.enter_context(tc.tile_pool(name="staging", bufs=6))
+        grouped = ctx.enter_context(tc.tile_pool(name="grouped", bufs=6))
+        staging = ctx.enter_context(tc.tile_pool(name="staging", bufs=4))
         psum = ctx.enter_context(tc.psum_pool(name="psum", bufs=8))
 
-        warm_in = consts.tile([P, 1], F32)
-        warm_out = consts.tile([P, 1], F32)
-        nc.vector.memset(warm_in[:], 0.0)
-        nc.scalar.activation(out=warm_out[:], in_=warm_in[:], func=IDENTITY)
+        zeros = consts.tile([P, 512], BF16)
+        nc.vector.memset(zeros[:].bitcast(I32), 0)
+        table = consts.tile([P, 1], F32)
+        nc.scalar.activation(out=table[:], in_=zeros[:, 0:1], func=IDENTITY)
         ident = consts.tile([P, P], F32)
         make_identity(nc, ident[:])
         bias_bf = consts.tile([P, NC * 8], BF16)
@@ -47,131 +46,139 @@ def tile_causalselfattention_pa_t_kernel(tc, x, Wk, pk_W, pk_b, out):
         nc.scalar.dma_start(out=bias_bf[:].rearrange("p (c j) -> p c j", c=NC),
                             in_=pk_b.rearrange("c (p j) -> p c j", j=8))
 
-        src = {}
-        for unit in [u for u in UNITS if u[0] in "WXP"]:
-            kind, n = unit[0], int(unit[1:] or 0)
-            raw = inputs.tile([P, 2048], BF16, name="raw_" + unit)
-            src[unit] = raw
-            if kind == "W":
-                nc.sync.dma_start(out=raw[:].rearrange("p (i c) -> p i c", i=4),
-                                  in_=Wk.rearrange("(i p) c -> p i c", p=P))
-            elif kind == "X":
-                b, c, g2 = (n // 2) % 2, n // 4, n % 2
-                t0 = N * c + 512 * g2
-                nc.sync.dma_start(out=raw[:].rearrange("p (a w) -> p a w", a=2),
-                                  in_=x[b, t0:t0 + 512, :].rearrange("(a p e) c -> p a (e c)", a=2, p=P, e=2))
-            else:
-                c, jj = n // 4, n % 4
-                nc.sync.dma_start(out=raw[:],
-                                  in_=pk_W[c].rearrange("(p j) n -> p (j n)", j=8)[:, 2048 * jj:2048 * jj + 2048])
-        codes = {}
-        scales = {}
-        groups = {}
-        results = {}
-        todo = [(unit, k) for unit in UNITS for k in range(4 if unit[0] == "K" else 2)]
-        filled = []
-        to_quantise = []
-        done = {"p": 0, "e": 0, "q": 0}
+        raw_w = inputs.tile([P, 2048], BF16)
+        nc.sync.dma_start(out=raw_w[:].rearrange("p (i c) -> p i c", i=4), in_=Wk.rearrange("(i p) c -> p i c", p=P))
+        raw_x = []
+        raw_pk = []
+        for g in range(GROUPS):
+            c, b, t0 = g // 4, (g // 2) % 2, 512 * (g % 2)
+            raw = inputs.tile([P, 2048], BF16, name="raw_x%d" % g)
+            nc.sync.dma_start(out=raw[:].rearrange("p (a w) -> p a w", a=2),
+                              in_=x[b, N * c + t0:N * c + t0 + 512, :].rearrange("(a p e) c -> p a (e c)", a=2, e=2))
+            raw_x.append(raw)
+            raw = inputs.tile([P, 2048], BF16, name="raw_pk%d" % g)
+            nc.sync.dma_start(out=raw[:], in_=pk_W[g // 4].rearrange("(p j) n -> p (j n)", j=8)[
+                :, 2048 * (g % 4):2048 * (g % 4) + 2048])
+            raw_pk.append(raw)
 
-        def fill(unit, k):
-            kind, n = unit[0], int(unit[1:] or 0)
-            if kind in "WXP":
+        issued = {"vector": 0, "scalar": 0}
+        waiting = []
+
+        def quantise_due():
+            while waiting and waiting[0][0] <= 0:
+                grp, codes, scales = waiting[0][1:]
+                waiting[:] = waiting[1:]
+                nc.vector.quantize_mx(out=codes[:].bitcast(FP8X4), scales=scales[:], in_=grp[:])
+                issued["vector"] += 1
+
+        def empty(dst, bank_view, add=None):
+            if issued["scalar"] <= issued["vector"] + len(waiting):
+                issued["scalar"] += 1
+                if add is None:
+                    nc.scalar.copy(out=dst, in_=bank_view)
+                else:
+                    nc.scalar.activation(out=dst, in_=bank_view, func=IDENTITY, bias=add, scale=1.0)
+            else:
+                issued["vector"] += 1
+                if add is None:
+                    nc.vector.tensor_copy(out=dst, in_=bank_view)
+                else:
+                    nc.vector.tensor_scalar_add(out=dst, in0=bank_view, scalar1=add)
+            for entry in waiting:
+                entry[0] -= 1
+            quantise_due()
+
+        def operand(label):
+            grp = grouped.tile([P, 2048], BF16, name="grp", tag="grp", align_bytes=64)
+            codes = keep.tile([P, 512], U32, name="codes_" + label, align_bytes=64)
+            scales = keep.tile([P, 512], U8, name="scales_" + label, align_bytes=64)
+            return grp, codes, scales
+
+        def warm_up(passes):
+            bank = psum.tile([P, 4, P], F32, name="bank", tag="bank")
+            for i in range(passes):
+                nc.tensor.matmul(out=bank[:].rearrange("p s o -> p (s o)"), lhsT=zeros[:, 0:P], rhs=zeros[:],
+                                 start=True, stop=True)
+
+        def transposed(raw, label):
+            words = raw[:].bitcast(F32)
+            grp, codes, scales = operand(label)
+            banks = []
+            for k in range(2):
                 bank = psum.tile([P, 4, P], F32, name="bank", tag="bank")
                 for s in range(4):
                     col = 512 * k + 128 * s
-                    nc.tensor.transpose(bank[:, s, :], src[unit][:].bitcast(F32)[:, col:col + 128], ident[:])
-            elif kind == "K":
-                xq, xs, wq, ws = codes["X%d" % n], scales["X%d" % n], codes["W"], scales["W"]
+                    nc.tensor.transpose(bank[:, s, :], words[:, col:col + 128], ident[:])
+                banks.append(bank)
+            for k in range(2):
+                empty(grp[:].bitcast(F32)[:, 512 * k:512 * k + 512].rearrange("q (i o u) -> q i o u", i=2, u=2),
+                      banks[k][:].rearrange("q (i u) o -> q i o u", i=2))
+            waiting.append([LAG, grp, codes, scales])
+            return codes, scales
+
+        def projected(xq, wq, label):
+            grp, codes, scales = operand(label)
+            banks = []
+            for h in range(NH):
                 bank = psum.tile([P, 4, P], F32, name="bank", tag="bank")
                 for t in range(4):
                     nc.tensor.matmul_mx(out=bank[:, t, :],
-                                        lhsT=xq[:, 128 * t:128 * t + 128].bitcast(FP8X4),
-                                        lhsT_scale=xs[:, 128 * t:128 * t + 128],
-                                        rhs=wq[:, 128 * k:128 * k + 128].bitcast(FP8X4),
-                                        rhs_scale=ws[:, 128 * k:128 * k + 128],
+                                        lhsT=xq[0][:, 128 * t:128 * t + 128].bitcast(FP8X4),
+                                        lhsT_scale=xq[1][:, 128 * t:128 * t + 128],
+                                        rhs=wq[0][:, 128 * h:128 * h + 128].bitcast(FP8X4),
+                                        rhs_scale=wq[1][:, 128 * h:128 * h + 128],
                                         start=True, stop=True)
-            else:
-                c, jj, b = int(unit[1]), int(unit[2]), int(unit[3])
-                if not results:
-                    nc.vector.tensor_copy(out=bias[:], in_=bias_bf[:])
-                    results["bias"] = True
-                pq, ps = codes["P%d" % (4 * c + jj)], scales["P%d" % (4 * c + jj)]
-                bank = psum.tile([P, 512], F32, name="bank", tag="bank")
+                banks.append(bank)
+            for h in range(NH):
+                empty(grp[:, 512 * h:512 * h + 512].rearrange("p (d t) -> p d t", t=4),
+                      banks[h][:].rearrange("p t d -> p d t"))
+            waiting.append([LAG, grp, codes, scales])
+            return codes, scales
+
+        def mixed(pq, kh, res, c, j0):
+            banks = []
+            for k in range(2):
+                bank = psum.tile([P, 4, P], F32, name="bank", tag="bank")
                 for g2 in range(2):
-                    kh = "K%d" % (2 * (2 * c + b) + g2)
                     col = 256 * k + 128 * g2
-                    nc.tensor.matmul_mx(out=bank[:],
-                                        lhsT=pq[:, col:col + 128].bitcast(FP8X4),
-                                        lhsT_scale=ps[:, col:col + 128],
-                                        rhs=codes[kh][:].bitcast(FP8X4),
-                                        rhs_scale=scales[kh][:],
+                    nc.tensor.matmul_mx(out=bank[:].rearrange("p h d -> p (h d)"),
+                                        lhsT=pq[0][:, col:col + 128].bitcast(FP8X4),
+                                        lhsT_scale=pq[1][:, col:col + 128],
+                                        rhs=kh[g2][0][:].bitcast(FP8X4),
+                                        rhs_scale=kh[g2][1][:],
                                         start=(g2 == 0), stop=(g2 == 1))
-            filled.append((unit, k, bank))
+                banks.append(bank)
+            for k in range(2):
+                j = j0 + k
+                empty(res[:, :, j % 4, :], banks[k][:], add=bias[:, 8 * c + j:8 * c + j + 1])
 
-        def copy(eng, dst, srcap):
-            if eng == "v":
-                nc.vector.tensor_copy(out=dst, in_=srcap)
-            else:
-                nc.scalar.copy(out=dst, in_=srcap)
-
-        def empty(eng):
-            unit, k, bank = filled[done["e"]]
-            done["e"] += 1
-            kind = unit[0]
-            if kind in "WXPK":
-                if k == 0:
-                    grp = grouped.tile([P, 2048], BF16, name="grp", tag="grp", align_bytes=64)
-                    groups[unit] = grp
-                grp = groups[unit]
-                if kind == "K":
-                    copy(eng, grp[:, 512 * k:512 * k + 512].rearrange("p (d t) -> p d t", t=4),
-                         bank[:].rearrange("p t d -> p d t"))
-                    if k == 3:
-                        to_quantise.append(unit)
-                else:
-                    copy(eng, grp[:].bitcast(F32)[:, 512 * k:512 * k + 512].rearrange("q (i o u) -> q i o u", i=2, u=2),
-                         bank[:].rearrange("q (i u) o -> q i o u", i=2))
-                    if k == 1:
-                        to_quantise.append(unit)
-                return
-            c, jj, b = int(unit[1]), int(unit[2]), int(unit[3])
-            half = jj // 2
-            key = (c, b, half)
-            if key not in results:
+        xq = []
+        pq = []
+        kq = []
+        warm_up(6)
+        wq = transposed(raw_w, "w")
+        warm_up(2)
+        for r in range(ROUNDS):
+            if r < GROUPS:
+                xq.append(transposed(raw_x[r], "x%d" % r))
+                if r == 0:
+                    warm_up(2)
+                pq.append(transposed(raw_pk[r], "pk%d" % r))
+                if r == 0:
+                    warm_up(2)
+            if r == FIRST_MIX:
+                nc.vector.tensor_copy(out=bias[:], in_=bias_bf[:])
+            if r >= FIRST_MIX:
+                block, half = (r - FIRST_MIX) // 2, (r - FIRST_MIX) % 2
+                c, b = block // 2, block % 2
                 res = staging.tile([P, NH, 4, HS], F32, name="res", tag="res")
-                results[key] = [res, 0]
-            res = results[key][0]
-            results[key][1] += 1
-            j = 2 * jj + k
-            acc = bank[:].rearrange("p (h d) -> p h d", h=NH)
-            col = 8 * c + j
-            if eng == "v":
-                nc.vector.tensor_scalar_add(out=res[:, :, j % 4, :], in0=acc, scalar1=bias[:, col:col + 1])
-            else:
-                nc.scalar.activation(out=res[:, :, j % 4, :], in_=acc, func=IDENTITY,
-                                     bias=bias[:, col:col + 1], scale=1.0)
-            dst = out[b, :, N * c:N * c + N, :].rearrange("h (p j) d -> p h j d", j=8)
-            if unit in PAIR_STORES:
-                if k == 1:
-                    lo = 2 * (jj % 2)
-                    nc.sync.dma_start(out=dst[:, :, 2 * jj:2 * jj + 2, :], in_=res[:, :, lo:lo + 2, :])
-            elif results[key][1] == 4:
-                nc.sync.dma_start(out=dst[:, :, 4 * half:4 * half + 4, :], in_=res[:])
-
-        def quantise():
-            unit = to_quantise[done["q"]]
-            done["q"] += 1
-            cw = keep.tile([P, 512], U32, name="codes_" + unit, align_bytes=64)
-            sc = keep.tile([P, 512], U8, name="scales_" + unit, align_bytes=64)
-            nc.vector.quantize_mx(out=cw[:].bitcast(FP8X4), scales=sc[:], in_=groups[unit][:])
-            codes[unit] = cw
-            scales[unit] = sc
-
-        for step in STEPS:
-            if step == "p":
-                fill(todo[done["p"]][0], todo[done["p"]][1])
-                done["p"] += 1
-            elif step == "q":
-                quantise()
-            else:
-                empty(step)
+                dst = out[b, :, N * c:N * c + N, :].rearrange("h (p j) d -> p h j d", j=8)
+                for i in range(2):
+                    j0 = 4 * half + 2 * i
+                    mixed(pq[4 * c + j0 // 2], kq[2 * block:2 * block + 2], res, c, j0)
+                    if r == ROUNDS - 1:
+                        nc.sync.dma_start(out=dst[:, :, j0:j0 + 2, :], in_=res[:, :, 2 * i:2 * i + 2, :])
+                if r < ROUNDS - 1:
+                    nc.sync.dma_start(out=dst[:, :, 4 * half:4 * half + 4, :], in_=res[:])
+            if 1 <= r <= GROUPS:
+                kq.append(projected(xq[r - 1], wq, "kh%d" % (r - 1)))

@@ -94,12 +94,6 @@ def tile_causalselfattention_pa_t_kernel(tc, x, Wk, pk_W, pk_b, out):
             scales = keep.tile([P, 512], U8, name="scales_" + label, align_bytes=64)
             return grp, codes, scales
 
-        def warm_up(passes):
-            bank = psum.tile([P, 4, P], F32, name="bank", tag="bank")
-            for i in range(passes):
-                nc.tensor.matmul(out=bank[:].rearrange("p s o -> p (s o)"), lhsT=zeros[:, 0:P], rhs=zeros[:],
-                                 start=True, stop=True)
-
         def transposed(raw, label):
             words = raw[:].bitcast(F32)
             grp, codes, scales = operand(label)
@@ -155,17 +149,11 @@ def tile_causalselfattention_pa_t_kernel(tc, x, Wk, pk_W, pk_b, out):
         xq = []
         pq = []
         kq = []
-        warm_up(6)
         wq = transposed(raw_w, "w")
-        warm_up(2)
         for r in range(ROUNDS):
             if r < GROUPS:
                 xq.append(transposed(raw_x[r], "x%d" % r))
-                if r == 0:
-                    warm_up(2)
                 pq.append(transposed(raw_pk[r], "pk%d" % r))
-                if r == 0:
-                    warm_up(2)
             if r == FIRST_MIX:
                 nc.vector.tensor_copy(out=bias[:], in_=bias_bf[:])
             if r >= FIRST_MIX:

@@ -27,7 +27,6 @@ LAG = 2
 def tile_causalselfattention_pa_t_kernel(tc, x, Wk, pk_W, pk_b, out):
     nc = tc.nc
     with ExitStack() as ctx:
-        ctx.enter_context(tc.manual_schedule())
         consts = ctx.enter_context(tc.tile_pool(name="consts", bufs=1))
         inputs = ctx.enter_context(tc.tile_pool(name="inputs", bufs=1))
         keep = ctx.enter_context(tc.tile_pool(name="keep", bufs=1))

@@ -5,7 +5,6 @@ from concourse.masks import make_identity
 
 F32 = mybir.dt.float32
 BF16 = mybir.dt.bfloat16
-I32 = mybir.dt.int32
 U32 = mybir.dt.uint32
 U8 = mybir.dt.uint8
 FP8X4 = mybir.dt.float8_e4m3fn_x4
@@ -17,33 +16,34 @@ HS = C // NH
 N = T // NC
 FLOPS = 2 * B * T * C * C + 2 * B * NH * NC * N * N * HS
 
-GROUPS = 8
-MIXES = 16
+GROUPS = B * T // 512
+ROWS = 8
 FIRST_MIX = 4
-ROUNDS = FIRST_MIX + MIXES // 2
+ROUNDS = FIRST_MIX + GROUPS
 LAG = 2
 
 
 def tile_causalselfattention_pa_t_kernel(tc, x, Wk, pk_W, pk_b, out):
     nc = tc.nc
     with ExitStack() as ctx:
+        ctx.enter_context(tc.manual_schedule())
         consts = ctx.enter_context(tc.tile_pool(name="consts", bufs=1))
         inputs = ctx.enter_context(tc.tile_pool(name="inputs", bufs=1))
         keep = ctx.enter_context(tc.tile_pool(name="keep", bufs=1))
-        grouped = ctx.enter_context(tc.tile_pool(name="grouped", bufs=6))
-        staging = ctx.enter_context(tc.tile_pool(name="staging", bufs=4))
+        grouped = ctx.enter_context(tc.tile_pool(name="grouped", bufs=4))
+        staging = ctx.enter_context(tc.tile_pool(name="staging", bufs=8))
         psum = ctx.enter_context(tc.psum_pool(name="psum", bufs=8))
 
-        zeros = consts.tile([P, 512], BF16)
-        nc.vector.memset(zeros[:].bitcast(I32), 0)
-        table = consts.tile([P, 1], F32)
-        nc.scalar.activation(out=table[:], in_=zeros[:, 0:1], func=IDENTITY)
+        scratch_in = consts.tile([P, 1], F32)
+        scratch_out = consts.tile([P, 1], F32)
+        nc.vector.memset(scratch_in[:], 0.0)
+        nc.scalar.activation(out=scratch_out[:], in_=scratch_in[:], func=IDENTITY)
         ident = consts.tile([P, P], F32)
         make_identity(nc, ident[:])
-        bias_bf = consts.tile([P, NC * 8], BF16)
-        bias = consts.tile([P, NC * 8], F32)
+        bias_bf = consts.tile([P, NC * ROWS], BF16)
+        bias = consts.tile([P, NC * ROWS], F32)
         nc.scalar.dma_start(out=bias_bf[:].rearrange("p (c j) -> p c j", c=NC),
-                            in_=pk_b.rearrange("c (p j) -> p c j", j=8))
+                            in_=pk_b.rearrange("c (p j) -> p c j", j=ROWS))
 
         raw_w = inputs.tile([P, 2048], BF16)
         nc.sync.dma_start(out=raw_w[:].rearrange("p (i c) -> p i c", i=4), in_=Wk.rearrange("(i p) c -> p i c", p=P))
@@ -56,8 +56,8 @@ def tile_causalselfattention_pa_t_kernel(tc, x, Wk, pk_W, pk_b, out):
                               in_=x[b, N * c + t0:N * c + t0 + 512, :].rearrange("(a p e) c -> p a (e c)", a=2, e=2))
             raw_x.append(raw)
             raw = inputs.tile([P, 2048], BF16, name="raw_pk%d" % g)
-            nc.sync.dma_start(out=raw[:], in_=pk_W[g // 4].rearrange("(p j) n -> p (j n)", j=8)[
-                :, 2048 * (g % 4):2048 * (g % 4) + 2048])
+            flat = pk_W[g // 4].rearrange("(p j) n -> p (j n)", j=ROWS)
+            nc.sync.dma_start(out=raw[:], in_=flat[:, 2048 * (g % 4):2048 * (g % 4) + 2048])
             raw_pk.append(raw)
 
         issued = {"vector": 0, "scalar": 0}
@@ -97,19 +97,19 @@ def tile_causalselfattention_pa_t_kernel(tc, x, Wk, pk_W, pk_b, out):
             words = raw[:].bitcast(F32)
             grp, codes, scales = operand(label)
             banks = []
-            for k in range(2):
+            for k2 in range(2):
                 bank = psum.tile([P, 4, P], F32, name="bank", tag="bank")
-                for s in range(4):
-                    col = 512 * k + 128 * s
-                    nc.tensor.transpose(bank[:, s, :], words[:, col:col + 128], ident[:])
+                for v in range(4):
+                    col = 512 * k2 + 128 * v
+                    nc.tensor.transpose(bank[:, v, :], words[:, col:col + 128], ident[:])
                 banks.append(bank)
-            for k in range(2):
-                empty(grp[:].bitcast(F32)[:, 512 * k:512 * k + 512].rearrange("q (i o u) -> q i o u", i=2, u=2),
-                      banks[k][:].rearrange("q (i u) o -> q i o u", i=2))
+            for k2 in range(2):
+                empty(grp[:].bitcast(F32)[:, 512 * k2:512 * k2 + 512].rearrange("q (i o u) -> q i o u", i=2, u=2),
+                      banks[k2][:].rearrange("q (i u) o -> q i o u", i=2))
             waiting.append([LAG, grp, codes, scales])
             return codes, scales
 
-        def projected(xq, wq, label):
+        def projected(xq, label):
             grp, codes, scales = operand(label)
             banks = []
             for h in range(NH):
@@ -128,12 +128,12 @@ def tile_causalselfattention_pa_t_kernel(tc, x, Wk, pk_W, pk_b, out):
             waiting.append([LAG, grp, codes, scales])
             return codes, scales
 
-        def mixed(pq, kh, res, c, j0):
+        def mixed(pq, kh, c, b, j0):
             banks = []
-            for k in range(2):
-                bank = psum.tile([P, 4, P], F32, name="bank", tag="bank")
+            for k2 in range(2):
+                bank = psum.tile([P, NH, HS], F32, name="bank", tag="bank")
                 for g2 in range(2):
-                    col = 256 * k + 128 * g2
+                    col = 256 * k2 + 128 * g2
                     nc.tensor.matmul_mx(out=bank[:].rearrange("p h d -> p (h d)"),
                                         lhsT=pq[0][:, col:col + 128].bitcast(FP8X4),
                                         lhsT_scale=pq[1][:, col:col + 128],
@@ -141,14 +141,17 @@ def tile_causalselfattention_pa_t_kernel(tc, x, Wk, pk_W, pk_b, out):
                                         rhs_scale=kh[g2][1][:],
                                         start=(g2 == 0), stop=(g2 == 1))
                 banks.append(bank)
-            for k in range(2):
-                j = j0 + k
-                empty(res[:, :, j % 4, :], banks[k][:], add=bias[:, 8 * c + j:8 * c + j + 1])
+            res = staging.tile([P, NH, 2, HS], F32, name="res", tag="res")
+            for k2 in range(2):
+                col = ROWS * c + j0 + k2
+                empty(res[:, :, k2, :], banks[k2][:], add=bias[:, col:col + 1])
+            dst = out[b, :, N * c:N * c + N, :].rearrange("h (p j) d -> p h j d", j=ROWS)
+            nc.sync.dma_start(out=dst[:, :, j0:j0 + 2, :], in_=res[:])
 
+        wq = transposed(raw_w, "w")
         xq = []
         pq = []
         kq = []
-        wq = transposed(raw_w, "w")
         for r in range(ROUNDS):
             if r < GROUPS:
                 xq.append(transposed(raw_x[r], "x%d" % r))
@@ -156,16 +159,9 @@ def tile_causalselfattention_pa_t_kernel(tc, x, Wk, pk_W, pk_b, out):
             if r == FIRST_MIX:
                 nc.vector.tensor_copy(out=bias[:], in_=bias_bf[:])
             if r >= FIRST_MIX:
-                block, half = (r - FIRST_MIX) // 2, (r - FIRST_MIX) % 2
-                c, b = block // 2, block % 2
-                res = staging.tile([P, NH, 4, HS], F32, name="res", tag="res")
-                dst = out[b, :, N * c:N * c + N, :].rearrange("h (p j) d -> p h j d", j=8)
-                for i in range(2):
-                    j0 = 4 * half + 2 * i
-                    mixed(pq[4 * c + j0 // 2], kq[2 * block:2 * block + 2], res, c, j0)
-                    if r == ROUNDS - 1:
-                        nc.sync.dma_start(out=dst[:, :, j0:j0 + 2, :], in_=res[:, :, 2 * i:2 * i + 2, :])
-                if r < ROUNDS - 1:
-                    nc.sync.dma_start(out=dst[:, :, 4 * half:4 * half + 4, :], in_=res[:])
+                panel, half = (r - FIRST_MIX) // 2, (r - FIRST_MIX) % 2
+                c, b = panel // 2, panel % 2
+                for s in (2 * half, 2 * half + 1):
+                    mixed(pq[4 * c + s], kq[2 * panel:2 * panel + 2], c, b, 2 * s)
             if 1 <= r <= GROUPS:
-                kq.append(projected(xq[r - 1], wq, "kh%d" % (r - 1)))
+                kq.append(projected(xq[r - 1], "kh%d" % (r - 1)))

@@ -18,7 +18,7 @@ FLOPS = 2 * B * T * C * C + 2 * B * NH * NC * N * N * HS
 
 GROUPS = B * T // 512
 ROWS = 8
-FIRST_MIX = 4
+FIRST_MIX = 3
 ROUNDS = FIRST_MIX + GROUPS
 LAG = 2
 
@@ -156,6 +156,8 @@ def tile_causalselfattention_pa_t_kernel(tc, x, Wk, pk_W, pk_b, out):
             if r < GROUPS:
                 xq.append(transposed(raw_x[r], "x%d" % r))
                 pq.append(transposed(raw_pk[r], "pk%d" % r))
+            if 1 <= r <= GROUPS:
+                kq.append(projected(xq[r - 1], "kh%d" % (r - 1)))
             if r == FIRST_MIX:
                 nc.vector.tensor_copy(out=bias[:], in_=bias_bf[:])
             if r >= FIRST_MIX:
@@ -163,5 +165,3 @@ def tile_causalselfattention_pa_t_kernel(tc, x, Wk, pk_W, pk_b, out):
                 c, b = panel // 2, panel % 2
                 for s in (2 * half, 2 * half + 1):
                     mixed(pq[4 * c + s], kq[2 * panel:2 * panel + 2], c, b, 2 * s)
-            if 1 <= r <= GROUPS:
-                kq.append(projected(xq[r - 1], "kh%d" % (r - 1)))

@@ -70,16 +70,15 @@ def tile_causalselfattention_pa_t_kernel(tc, x, Wk, pk_W, pk_b, out):
                 nc.vector.quantize_mx(out=codes[:].bitcast(FP8X4), scales=scales[:], in_=grp[:])
                 issued["vector"] += 1
 
-        def empty(dst, bank_view, add=None):
-            if issued["scalar"] <= issued["vector"] + len(waiting):
-                issued["scalar"] += 1
-                if add is None:
+        def empty(pieces):
+            on_scalar = issued["scalar"] <= issued["vector"] + len(waiting)
+            issued["scalar" if on_scalar else "vector"] += 1
+            for dst, bank_view, add in pieces:
+                if on_scalar and add is None:
                     nc.scalar.copy(out=dst, in_=bank_view)
-                else:
+                elif on_scalar:
                     nc.scalar.activation(out=dst, in_=bank_view, func=IDENTITY, bias=add, scale=1.0)
-            else:
-                issued["vector"] += 1
-                if add is None:
+                elif add is None:
                     nc.vector.tensor_copy(out=dst, in_=bank_view)
                 else:
                     nc.vector.tensor_scalar_add(out=dst, in0=bank_view, scalar1=add)
@@ -104,8 +103,8 @@ def tile_causalselfattention_pa_t_kernel(tc, x, Wk, pk_W, pk_b, out):
                     nc.tensor.transpose(bank[:, v, :], words[:, col:col + 128], ident[:])
                 banks.append(bank)
             for k2 in range(2):
-                empty(grp[:].bitcast(F32)[:, 512 * k2:512 * k2 + 512].rearrange("q (i o u) -> q i o u", i=2, u=2),
-                      banks[k2][:].rearrange("q (i u) o -> q i o u", i=2))
+                empty([(grp[:].bitcast(F32)[:, 512 * k2:512 * k2 + 512].rearrange("q (i o u) -> q i o u", i=2, u=2),
+                        banks[k2][:].rearrange("q (i u) o -> q i o u", i=2), None)])
             waiting.append([LAG, grp, codes, scales])
             return codes, scales
 
@@ -123,8 +122,8 @@ def tile_causalselfattention_pa_t_kernel(tc, x, Wk, pk_W, pk_b, out):
                                         start=True, stop=True)
                 banks.append(bank)
             for h in range(NH):
-                empty(grp[:, 512 * h:512 * h + 512].rearrange("p (d t) -> p d t", t=4),
-                      banks[h][:].rearrange("p t d -> p d t"))
+                empty([(grp[:, 512 * h:512 * h + 512].rearrange("p (d t) -> p d t", t=4),
+                        banks[h][:].rearrange("p t d -> p d t"), None)])
             waiting.append([LAG, grp, codes, scales])
             return codes, scales
 
@@ -144,9 +143,32 @@ def tile_causalselfattention_pa_t_kernel(tc, x, Wk, pk_W, pk_b, out):
             res = staging.tile([P, NH, 2, HS], F32, name="res", tag="res")
             for k2 in range(2):
                 col = ROWS * c + j0 + k2
-                empty(res[:, :, k2, :], banks[k2][:], add=bias[:, col:col + 1])
+                empty([(res[:, :, k2, :], banks[k2][:], bias[:, col:col + 1])])
             dst = out[b, :, N * c:N * c + N, :].rearrange("h (p j) d -> p h j d", j=ROWS)
             nc.sync.dma_start(out=dst[:, :, j0:j0 + 2, :], in_=res[:])
+
+        def mixed_by_heads(pq2, kh, c, b, j0):
+            dst = out[b, :, N * c:N * c + N, :].rearrange("h (p j) d -> p h j d", j=ROWS)
+            for hp in range(2):
+                banks = []
+                for s in range(2):
+                    bank = psum.tile([P, 2, 2, HS], F32, name="bank", tag="bank")
+                    for k2 in range(2):
+                        for g2 in range(2):
+                            col = 256 * k2 + 128 * g2
+                            nc.tensor.matmul_mx(out=bank[:, k2, :, :].rearrange("p h d -> p (h d)"),
+                                                lhsT=pq2[s][0][:, col:col + 128].bitcast(FP8X4),
+                                                lhsT_scale=pq2[s][1][:, col:col + 128],
+                                                rhs=kh[g2][0][:, 256 * hp:256 * hp + 256].bitcast(FP8X4),
+                                                rhs_scale=kh[g2][1][:, 256 * hp:256 * hp + 256],
+                                                start=(g2 == 0), stop=(g2 == 1))
+                    banks.append(bank)
+                res = staging.tile([P, 2, 4, HS], F32, name="res", tag="res")
+                for s in range(2):
+                    col = ROWS * c + j0 + 2 * s
+                    empty([(res[:, :, 2 * s + k2, :], banks[s][:, k2, :, :], bias[:, col + k2:col + k2 + 1])
+                           for k2 in range(2)])
+                nc.sync.dma_start(out=dst[:, 2 * hp:2 * hp + 2, j0:j0 + 4, :], in_=res[:])
 
         wq = transposed(raw_w, "w")
         xq = []
@@ -163,5 +185,8 @@ def tile_causalselfattention_pa_t_kernel(tc, x, Wk, pk_W, pk_b, out):
             if r >= FIRST_MIX:
                 panel, half = (r - FIRST_MIX) // 2, (r - FIRST_MIX) % 2
                 c, b = panel // 2, panel % 2
-                for s in (2 * half, 2 * half + 1):
-                    mixed(pq[4 * c + s], kq[2 * panel:2 * panel + 2], c, b, 2 * s)
+                if r >= GROUPS:
+                    mixed_by_heads(pq[4 * c + 2 * half:4 * c + 2 * half + 2], kq[2 * panel:2 * panel + 2], c, b, 4 * half)
+                else:
+                    for s in (2 * half, 2 * half + 1):
+                        mixed(pq[4 * c + s], kq[2 * panel:2 * panel + 2], c, b, 2 * s)

@@ -42,11 +42,9 @@ def tile_causalselfattention_pa_t_kernel(tc, x, Wk, pk_W, pk_b, out):
         make_identity(nc, ident[:])
         bias_bf = consts.tile([P, NC * ROWS], BF16)
         bias = consts.tile([P, NC * ROWS], F32)
-        nc.scalar.dma_start(out=bias_bf[:].rearrange("p (c j) -> p c j", c=NC),
-                            in_=pk_b.rearrange("c (p j) -> p c j", j=ROWS))
 
         raw_w = inputs.tile([P, 2048], BF16)
-        nc.sync.dma_start(out=raw_w[:].rearrange("p (i c) -> p i c", i=4), in_=Wk.rearrange("(i p) c -> p i c", p=P))
+        nc.sync.dma_start(out=raw_w[:], in_=Wk.rearrange("(p i) c -> p (i c)", i=4))
         raw_x = []
         raw_pk = []
         for g in range(GROUPS):
@@ -59,6 +57,9 @@ def tile_causalselfattention_pa_t_kernel(tc, x, Wk, pk_W, pk_b, out):
             flat = pk_W[g // 4].rearrange("(p j) n -> p (j n)", j=ROWS)
             nc.sync.dma_start(out=raw[:], in_=flat[:, 2048 * (g % 4):2048 * (g % 4) + 2048])
             raw_pk.append(raw)
+            if g == 2:
+                nc.sync.dma_start(out=bias_bf[:].rearrange("p (c j) -> p c j", c=NC),
+                                  in_=pk_b.rearrange("c (p j) -> p c j", j=ROWS))
 
         issued = {"vector": 0, "scalar": 0}
         waiting = []
@@ -92,7 +93,7 @@ def tile_causalselfattention_pa_t_kernel(tc, x, Wk, pk_W, pk_b, out):
             scales = keep.tile([P, 512], U8, name="scales_" + label, align_bytes=64)
             return grp, codes, scales
 
-        def transposed(raw, label):
+        def transposed(raw, label, rows_apart=False):
             words = raw[:].bitcast(F32)
             grp, codes, scales = operand(label)
             banks = []
@@ -103,8 +104,12 @@ def tile_causalselfattention_pa_t_kernel(tc, x, Wk, pk_W, pk_b, out):
                     nc.tensor.transpose(bank[:, v, :], words[:, col:col + 128], ident[:])
                 banks.append(bank)
             for k2 in range(2):
-                empty([(grp[:].bitcast(F32)[:, 512 * k2:512 * k2 + 512].rearrange("q (i o u) -> q i o u", i=2, u=2),
-                        banks[k2][:].rearrange("q (i u) o -> q i o u", i=2), None)])
+                if rows_apart:
+                    empty([(grp[:].bitcast(F32).rearrange("q (o w) -> q o w", w=8)[:, :, 4 * k2:4 * k2 + 4],
+                            banks[k2][:].rearrange("q v o -> q o v"), None)])
+                else:
+                    empty([(grp[:].bitcast(F32)[:, 512 * k2:512 * k2 + 512].rearrange("q (i o u) -> q i o u", i=2, u=2),
+                            banks[k2][:].rearrange("q (i u) o -> q i o u", i=2), None)])
             waiting.append([LAG, grp, codes, scales])
             return codes, scales
 
@@ -170,7 +175,7 @@ def tile_causalselfattention_pa_t_kernel(tc, x, Wk, pk_W, pk_b, out):
                            for k2 in range(2)])
                 nc.sync.dma_start(out=dst[:, 2 * hp:2 * hp + 2, j0:j0 + 4, :], in_=res[:])
 
-        wq = transposed(raw_w, "w")
+        wq = transposed(raw_w, "w", rows_apart=True)
         xq = []
         pq = []
         kq = []

@@ -20,6 +20,7 @@ GROUPS = B * T // 512
 ROWS = 8
 FIRST_MIX = 3
 ROUNDS = FIRST_MIX + GROUPS
+PAD = 64
 LAG = 2
 
 
@@ -68,7 +69,7 @@ def tile_causalselfattention_pa_t_kernel(tc, x, Wk, pk_W, pk_b, out):
             while waiting and waiting[0][0] <= 0:
                 grp, codes, scales = waiting[0][1:]
                 waiting[:] = waiting[1:]
-                nc.vector.quantize_mx(out=codes[:].bitcast(FP8X4), scales=scales[:], in_=grp[:])
+                nc.vector.quantize_mx(out=codes[:].bitcast(FP8X4), scales=scales, in_=grp[:])
                 issued["vector"] += 1
 
         def empty(pieces):
@@ -89,9 +90,9 @@ def tile_causalselfattention_pa_t_kernel(tc, x, Wk, pk_W, pk_b, out):
 
         def operand(label):
             grp = grouped.tile([P, 2048], BF16, name="grp", tag="grp", align_bytes=64)
-            codes = keep.tile([P, 512], U32, name="codes_" + label, align_bytes=64)
-            scales = keep.tile([P, 512], U8, name="scales_" + label, align_bytes=64)
-            return grp, codes, scales
+            codes = keep.tile([P, 512], U32, name="codes_" + label, align_bytes=256)
+            padded = keep.tile([P, PAD + 512], U8, name="scales_" + label, align_bytes=256)
+            return grp, codes, padded[:, PAD:PAD + 512]
 
         def transposed(raw, label, rows_apart=False):
             words = raw[:].bitcast(F32)
@@ -142,7 +143,7 @@ def tile_causalselfattention_pa_t_kernel(tc, x, Wk, pk_W, pk_b, out):
                                         lhsT=pq[0][:, col:col + 128].bitcast(FP8X4),
                                         lhsT_scale=pq[1][:, col:col + 128],
                                         rhs=kh[g2][0][:].bitcast(FP8X4),
-                                        rhs_scale=kh[g2][1][:],
+                                        rhs_scale=kh[g2][1],
                                         start=(g2 == 0), stop=(g2 == 1))
                 banks.append(bank)
             res = staging.tile([P, NH, 2, HS], F32, name="res", tag="res")

@@ -69,7 +69,7 @@ def tile_causalselfattention_pa_t_kernel(tc, x, Wk, pk_W, pk_b, out):
             while waiting and waiting[0][0] <= 0:
                 grp, codes, scales = waiting[0][1:]
                 waiting[:] = waiting[1:]
-                nc.vector.quantize_mx(out=codes[:].bitcast(FP8X4), scales=scales, in_=grp[:])
+                nc.vector.quantize_mx(out=codes.bitcast(FP8X4), scales=scales, in_=grp[:])
                 issued["vector"] += 1
 
         def empty(pieces):
@@ -88,15 +88,16 @@ def tile_causalselfattention_pa_t_kernel(tc, x, Wk, pk_W, pk_b, out):
                 entry[0] -= 1
             quantise_due()
 
-        def operand(label):
+        def operand(label, moving=False):
             grp = grouped.tile([P, 2048], BF16, name="grp", tag="grp", align_bytes=64)
-            codes = keep.tile([P, 512], U32, name="codes_" + label, align_bytes=256)
-            padded = keep.tile([P, PAD + 512], U8, name="scales_" + label, align_bytes=256)
-            return grp, codes, padded[:, PAD:PAD + 512]
+            shift = 128 if moving else 0
+            wide = keep.tile([P, shift // 4 + 512], U32, name="codes_" + label, align_bytes=256)
+            padded = keep.tile([P, shift + PAD + 512], U8, name="scales_" + label, align_bytes=256)
+            return grp, wide[:, shift // 4:shift // 4 + 512], padded[:, shift + PAD:shift + PAD + 512]
 
         def transposed(raw, label, rows_apart=False):
             words = raw[:].bitcast(F32)
-            grp, codes, scales = operand(label)
+            grp, codes, scales = operand(label, moving=rows_apart)
             banks = []
             for k2 in range(2):
                 bank = psum.tile([P, 4, P], F32, name="bank", tag="bank")
@@ -115,7 +116,7 @@ def tile_causalselfattention_pa_t_kernel(tc, x, Wk, pk_W, pk_b, out):
             return codes, scales
 
         def projected(xq, label):
-            grp, codes, scales = operand(label)
+            grp, codes, scales = operand(label, moving=True)
             banks = []
             for h in range(NH):
                 bank = psum.tile([P, 4, P], F32, name="bank", tag="bank")
@@ -142,7 +143,7 @@ def tile_causalselfattention_pa_t_kernel(tc, x, Wk, pk_W, pk_b, out):
                     nc.tensor.matmul_mx(out=bank[:].rearrange("p h d -> p (h d)"),
                                         lhsT=pq[0][:, col:col + 128].bitcast(FP8X4),
                                         lhsT_scale=pq[1][:, col:col + 128],
-                                        rhs=kh[g2][0][:].bitcast(FP8X4),
+                                        rhs=kh[g2][0].bitcast(FP8X4),
                                         rhs_scale=kh[g2][1],
                                         start=(g2 == 0), stop=(g2 == 1))
                 banks.append(bank)

from contextlib import ExitStack

import concourse.mybir as mybir
from concourse.masks import make_identity

F32 = mybir.dt.float32
BF16 = mybir.dt.bfloat16
U32 = mybir.dt.uint32
U8 = mybir.dt.uint8
FP8X4 = mybir.dt.float8_e4m3fn_x4
IDENTITY = mybir.ActivationFunctionType.Identity

P = 128
B, T, C, NH, NC = 2, 2048, 512, 4, 2
HS = C // NH
N = T // NC
FLOPS = 2 * B * T * C * C + 2 * B * NH * NC * N * N * HS

GROUPS = B * T // 512
ROWS = 8
FIRST_MIX = 3
ROUNDS = FIRST_MIX + GROUPS
PAD = 64
LAG = 2


def tile_causalselfattention_pa_t_kernel(tc, x, Wk, pk_W, pk_b, out):
    nc = tc.nc
    with ExitStack() as ctx:
        ctx.enter_context(tc.manual_schedule())
        consts = ctx.enter_context(tc.tile_pool(name="consts", bufs=1))
        inputs = ctx.enter_context(tc.tile_pool(name="inputs", bufs=1))
        keep = ctx.enter_context(tc.tile_pool(name="keep", bufs=1))
        grouped = ctx.enter_context(tc.tile_pool(name="grouped", bufs=4))
        staging = ctx.enter_context(tc.tile_pool(name="staging", bufs=8))
        psum = ctx.enter_context(tc.psum_pool(name="psum", bufs=8))

        scratch_in = consts.tile([P, 1], F32)
        scratch_out = consts.tile([P, 1], F32)
        nc.vector.memset(scratch_in[:], 0.0)
        nc.scalar.activation(out=scratch_out[:], in_=scratch_in[:], func=IDENTITY)
        ident = consts.tile([P, P], F32)
        make_identity(nc, ident[:])
        bias_bf = consts.tile([P, NC * ROWS], BF16)
        bias = consts.tile([P, NC * ROWS], F32)

        raw_w = inputs.tile([P, 2048], BF16)
        nc.sync.dma_start(out=raw_w[:], in_=Wk.rearrange("(p i) c -> p (i c)", i=4))
        raw_x = []
        raw_pk = []
        for g in range(GROUPS):
            c, b, t0 = g // 4, (g // 2) % 2, 512 * (g % 2)
            raw = inputs.tile([P, 2048], BF16, name="raw_x%d" % g)
            nc.sync.dma_start(out=raw[:].rearrange("p (a w) -> p a w", a=2),
                              in_=x[b, N * c + t0:N * c + t0 + 512, :].rearrange("(a p e) c -> p a (e c)", a=2, e=2))
            raw_x.append(raw)
            raw = inputs.tile([P, 2048], BF16, name="raw_pk%d" % g)
            flat = pk_W[g // 4].rearrange("(p j) n -> p (j n)", j=ROWS)
            nc.sync.dma_start(out=raw[:], in_=flat[:, 2048 * (g % 4):2048 * (g % 4) + 2048])
            raw_pk.append(raw)
            if g == 2:
                nc.sync.dma_start(out=bias_bf[:].rearrange("p (c j) -> p c j", c=NC),
                                  in_=pk_b.rearrange("c (p j) -> p c j", j=ROWS))

        issued = {"vector": 0, "scalar": 0}
        waiting = []

        def quantise_due():
            while waiting and waiting[0][0] <= 0:
                grp, codes, scales = waiting[0][1:]
                waiting[:] = waiting[1:]
                nc.vector.quantize_mx(out=codes.bitcast(FP8X4), scales=scales, in_=grp[:])
                issued["vector"] += 1

        def empty(pieces):
            on_scalar = issued["scalar"] <= issued["vector"] + len(waiting)
            issued["scalar" if on_scalar else "vector"] += 1
            for dst, bank_view, add in pieces:
                if on_scalar and add is None:
                    nc.scalar.copy(out=dst, in_=bank_view)
                elif on_scalar:
                    nc.scalar.activation(out=dst, in_=bank_view, func=IDENTITY, bias=add, scale=1.0)
                elif add is None:
                    nc.vector.tensor_copy(out=dst, in_=bank_view)
                else:
                    nc.vector.tensor_scalar_add(out=dst, in0=bank_view, scalar1=add)
            for entry in waiting:
                entry[0] -= 1
            quantise_due()

        def operand(label, moving=False):
            grp = grouped.tile([P, 2048], BF16, name="grp", tag="grp", align_bytes=64)
            shift = 128 if moving else 0
            wide = keep.tile([P, shift // 4 + 512], U32, name="codes_" + label, align_bytes=256)
            padded = keep.tile([P, shift + PAD + 512], U8, name="scales_" + label, align_bytes=256)
            return grp, wide[:, shift // 4:shift // 4 + 512], padded[:, shift + PAD:shift + PAD + 512]

        def transposed(raw, label, rows_apart=False):
            words = raw[:].bitcast(F32)
            grp, codes, scales = operand(label, moving=rows_apart)
            banks = []
            for k2 in range(2):
                bank = psum.tile([P, 4, P], F32, name="bank", tag="bank")
                for v in range(4):
                    col = 512 * k2 + 128 * v
                    nc.tensor.transpose(bank[:, v, :], words[:, col:col + 128], ident[:])
                banks.append(bank)
            for k2 in range(2):
                if rows_apart:
                    empty([(grp[:].bitcast(F32).rearrange("q (o w) -> q o w", w=8)[:, :, 4 * k2:4 * k2 + 4],
                            banks[k2][:].rearrange("q v o -> q o v"), None)])
                else:
                    empty([(grp[:].bitcast(F32)[:, 512 * k2:512 * k2 + 512].rearrange("q (i o u) -> q i o u", i=2, u=2),
                            banks[k2][:].rearrange("q (i u) o -> q i o u", i=2), None)])
            waiting.append([LAG, grp, codes, scales])
            return codes, scales

        def projected(xq, label):
            grp, codes, scales = operand(label, moving=True)
            banks = []
            for h in range(NH):
                bank = psum.tile([P, 4, P], F32, name="bank", tag="bank")
                for t in range(4):
                    nc.tensor.matmul_mx(out=bank[:, t, :],
                                        lhsT=xq[0][:, 128 * t:128 * t + 128].bitcast(FP8X4),
                                        lhsT_scale=xq[1][:, 128 * t:128 * t + 128],
                                        rhs=wq[0][:, 128 * h:128 * h + 128].bitcast(FP8X4),
                                        rhs_scale=wq[1][:, 128 * h:128 * h + 128],
                                        start=True, stop=True)
                banks.append(bank)
            for h in range(NH):
                empty([(grp[:, 512 * h:512 * h + 512].rearrange("p (d t) -> p d t", t=4),
                        banks[h][:].rearrange("p t d -> p d t"), None)])
            waiting.append([LAG, grp, codes, scales])
            return codes, scales

        def mixed(pq, kh, c, b, j0):
            banks = []
            for k2 in range(2):
                bank = psum.tile([P, NH, HS], F32, name="bank", tag="bank")
                for g2 in range(2):
                    col = 256 * k2 + 128 * g2
                    nc.tensor.matmul_mx(out=bank[:].rearrange("p h d -> p (h d)"),
                                        lhsT=pq[0][:, col:col + 128].bitcast(FP8X4),
                                        lhsT_scale=pq[1][:, col:col + 128],
                                        rhs=kh[g2][0].bitcast(FP8X4),
                                        rhs_scale=kh[g2][1],
                                        start=(g2 == 0), stop=(g2 == 1))
                banks.append(bank)
            res = staging.tile([P, NH, 2, HS], F32, name="res", tag="res")
            for k2 in range(2):
                col = ROWS * c + j0 + k2
                empty([(res[:, :, k2, :], banks[k2][:], bias[:, col:col + 1])])
            dst = out[b, :, N * c:N * c + N, :].rearrange("h (p j) d -> p h j d", j=ROWS)
            nc.sync.dma_start(out=dst[:, :, j0:j0 + 2, :], in_=res[:])

        def mixed_by_heads(pq2, kh, c, b, j0):
            dst = out[b, :, N * c:N * c + N, :].rearrange("h (p j) d -> p h j d", j=ROWS)
            for hp in range(2):
                banks = []
                for s in range(2):
                    bank = psum.tile([P, 2, 2, HS], F32, name="bank", tag="bank")
                    for k2 in range(2):
                        for g2 in range(2):
                            col = 256 * k2 + 128 * g2
                            nc.tensor.matmul_mx(out=bank[:, k2, :, :].rearrange("p h d -> p (h d)"),
                                                lhsT=pq2[s][0][:, col:col + 128].bitcast(FP8X4),
                                                lhsT_scale=pq2[s][1][:, col:col + 128],
                                                rhs=kh[g2][0][:, 256 * hp:256 * hp + 256].bitcast(FP8X4),
                                                rhs_scale=kh[g2][1][:, 256 * hp:256 * hp + 256],
                                                start=(g2 == 0), stop=(g2 == 1))
                    banks.append(bank)
                res = staging.tile([P, 2, 4, HS], F32, name="res", tag="res")
                for s in range(2):
                    col = ROWS * c + j0 + 2 * s
                    empty([(res[:, :, 2 * s + k2, :], banks[s][:, k2, :, :], bias[:, col + k2:col + k2 + 1])
                           for k2 in range(2)])
                nc.sync.dma_start(out=dst[:, 2 * hp:2 * hp + 2, j0:j0 + 4, :], in_=res[:])

        wq = transposed(raw_w, "w", rows_apart=True)
        xq = []
        pq = []
        kq = []
        for r in range(ROUNDS):
            if r < GROUPS:
                xq.append(transposed(raw_x[r], "x%d" % r))
                pq.append(transposed(raw_pk[r], "pk%d" % r))
            if 1 <= r <= GROUPS:
                kq.append(projected(xq[r - 1], "kh%d" % (r - 1)))
            if r == FIRST_MIX:
                nc.vector.tensor_copy(out=bias[:], in_=bias_bf[:])
            if r >= FIRST_MIX:
                panel, half = (r - FIRST_MIX) // 2, (r - FIRST_MIX) % 2
                c, b = panel // 2, panel % 2
                if r >= GROUPS:
                    mixed_by_heads(pq[4 * c + 2 * half:4 * c + 2 * half + 2], kq[2 * panel:2 * panel + 2], c, b, 4 * half)
                else:
                    for s in (2 * half, 2 * half + 1):
                        mixed(pq[4 * c + s], kq[2 * panel:2 * panel + 2], c, b, 2 * s)
